import numpy as np
import ml_dtypes


def mxq(x, axis, fmt="e4m3"):
    dtype, down = {"e4m3": (ml_dtypes.float8_e4m3fn, 7), "e5m2": (ml_dtypes.float8_e5m2, 14)}[fmt]
    v = np.moveaxis(np.asarray(x, np.float32).astype(ml_dtypes.bfloat16).astype(np.float64), axis, -1)
    blocks = v.reshape(v.shape[:-1] + (-1, 32))
    amax = np.abs(blocks).max(-1, keepdims=True)
    byte = np.maximum(np.where(amax > 0, np.frexp(amax)[1] - 1 + 127, 0) - down, 1)
    scale = np.exp2(byte - 127.0)
    codes = (blocks / scale).astype(np.float32).astype(dtype).astype(np.float64)
    return np.moveaxis((codes * scale).reshape(v.shape), -1, axis)


WIDE = False


def mx_kscale(k):
    if not WIDE:
        return np.ones(k)
    levels = np.array([10, -10, 5, -5, 0])
    a = np.random.permutation(np.resize(levels, k // 512 * 4)).reshape(k // 512, 4)
    idx = np.arange(k)
    return np.exp2(a[idx // 512, idx % 128 // 32])


BF16 = ml_dtypes.bfloat16


def bf(x):
    return np.asarray(x, np.float32).astype(BF16)


def f64(x):
    return np.asarray(x).astype(np.float64)


B, N, C = 8, 512, 512
R = B * N
G = 3 * C


def sigmoid(v):
    return 1.0 / (1.0 + np.exp(-v))


def setup_inputs():
    s = mx_kscale(C)
    s = s / s.max()
    return {"x_proj": bf(np.random.standard_normal((R, G))),
            "annotations": bf(np.random.standard_normal((B, N, C)) * s),
            "recurrent_kernel": bf(np.random.standard_normal((C, G)) / np.sqrt(C) / s[:, None]),
            "bias_h": bf(np.random.standard_normal(G) * 0.3)}


def reference(x_proj, annotations, recurrent_kernel, bias_h):
    b, n, c = annotations.shape
    h = f64(annotations).reshape(-1, c)
    mh = (mxq(h, 1, "e4m3") @ mxq(f64(recurrent_kernel), 0, "e4m3")) + f64(bias_h)
    xz, xr, xh = np.split(f64(x_proj), 3, axis=-1)
    hz, hr, hh_in = np.split(mh, 3, axis=-1)
    z = sigmoid(xz + hz)
    r = sigmoid(xr + hr)
    hh = np.tanh(xh + r * hh_in)
    out = z * h + (1.0 - z) * hh
    return out.reshape(b, n, c)

@@ -1,0 +1,129 @@
+from contextlib import ExitStack
+
+import concourse.mybir as mybir
+from concourse.masks import make_identity
+
+F32 = mybir.dt.float32
+BF16 = mybir.dt.bfloat16
+U32 = mybir.dt.uint32
+U8 = mybir.dt.uint8
+FP8X4 = mybir.dt.float8_e4m3fn_x4
+ALU = mybir.AluOpType
+FN = mybir.ActivationFunctionType
+
+P = 128
+C = 512
+G = 3 * C
+R = 4096
+TPB = 4
+BLOCK = P * TPB
+NBLK = R // BLOCK
+
+FLOPS = 2 * R * C * G
+
+
+def tile_gatedgraphconvolution_pb_t_kernel(tc, x_proj, annotations, recurrent_kernel, bias_h, out):
+    nc = tc.nc
+    h_all = annotations.flatten_outer_dims()
+    out_all = out.flatten_outer_dims()
+
+    with ExitStack() as ctx:
+        const = ctx.enter_context(tc.tile_pool(name="const", bufs=1))
+        xpool = ctx.enter_context(tc.tile_pool(name="xpool", bufs=3))
+        hpool = ctx.enter_context(tc.tile_pool(name="hpool", bufs=3))
+        qpool = ctx.enter_context(tc.tile_pool(name="qpool", bufs=2))
+        work = ctx.enter_context(tc.tile_pool(name="work", bufs=4))
+        opool = ctx.enter_context(tc.tile_pool(name="opool", bufs=3))
+        ps_t = ctx.enter_context(tc.psum_pool(name="ps_t", bufs=2))
+        ps_m = ctx.enter_context(tc.psum_pool(name="ps_m", bufs=6))
+
+        ident = const.tile([P, P], F32)
+        make_identity(nc, ident[:])
+
+        w_raw = const.tile([P, 4, G], BF16)
+        for u in range(2):
+            nc.sync.dma_start(
+                out=w_raw[:, 2 * u : 2 * u + 2, :],
+                in_=recurrent_kernel[256 * u : 256 * u + 256, :].rearrange("(q e) c -> q e c", e=2),
+            )
+        b_bc = const.tile([P, G], BF16)
+        nc.scalar.dma_start(out=b_bc[:], in_=bias_h.partition_broadcast(P))
+
+        w_grp = const.tile([P, G, 4], BF16, align_bytes=64)
+        w_codes = const.tile([P, G], U32, align_bytes=64)
+        w_scales = const.tile([P, G], U8, align_bytes=64)
+        for g in range(3):
+            cs = slice(C * g, C * g + C)
+            nc.vector.tensor_copy(out=w_grp[:, cs, :], in_=w_raw[:, :, cs].rearrange("q t c -> q c t"))
+        for g in range(3):
+            cs = slice(C * g, C * g + C)
+            nc.vector.quantize_mx(
+                out=w_codes[:, cs].bitcast(FP8X4),
+                scales=w_scales[:, cs],
+                in_=w_grp[:, cs, :].rearrange("q c t -> q (c t)"),
+            )
+
+        for b in range(NBLK):
+            rows = slice(BLOCK * b, BLOCK * b + BLOCK)
+            h_blk = hpool.tile([P, TPB * C], BF16)
+            nc.sync.dma_start(out=h_blk[:], in_=h_all[rows, :].rearrange("(p t) c -> p (t c)", t=TPB))
+            x_blk = xpool.tile([P, TPB * G], BF16)
+            nc.sync.dma_start(out=x_blk[:], in_=x_proj[rows, :].rearrange("(p t) c -> p (t c)", t=TPB))
+
+            h_words = h_blk[:].bitcast(F32)
+            h_grp = qpool.tile([P, 4 * BLOCK], BF16, align_bytes=64)
+            h_grp_w = h_grp[:].bitcast(F32).rearrange("q (t p u) -> q t p u", t=TPB, u=2)
+            for half in range(2):
+                xt = ps_t.tile([P, 4, P], F32)
+                for j in range(4):
+                    t = 2 * half + j // 2
+                    u = j % 2
+                    nc.tensor.transpose(xt[:, j, :], h_words[:, 256 * t + P * u : 256 * t + P * u + P], ident[:])
+                nc.scalar.copy(
+                    out=h_grp_w[:, 2 * half : 2 * half + 2, :, :],
+                    in_=xt[:].rearrange("q (t u) p -> q t p u", u=2),
+                )
+            h_codes = qpool.tile([P, BLOCK], U32, align_bytes=64)
+            h_scales = qpool.tile([P, BLOCK], U8, align_bytes=64)
+            nc.vector.quantize_mx(out=h_codes[:].bitcast(FP8X4), scales=h_scales[:], in_=h_grp[:])
+
+            o_blk = opool.tile([P, TPB * C], F32)
+            for t in range(TPB):
+                ns = slice(P * t, P * t + P)
+                acc = []
+                for g in range(3):
+                    cs = slice(C * g, C * g + C)
+                    pg = ps_m.tile([P, C], F32, name="pg", tag="pg")
+                    nc.tensor.matmul_mx(
+                        out=pg[:],
+                        lhsT=h_codes[:, ns].bitcast(FP8X4),
+                        lhsT_scale=h_scales[:, ns],
+                        rhs=w_codes[:, cs].bitcast(FP8X4),
+                        rhs_scale=w_scales[:, cs],
+                        start=True,
+                        stop=True,
+                    )
+                    acc.append(pg)
+                xz = x_blk[:, G * t : G * t + C]
+                xr = x_blk[:, G * t + C : G * t + 2 * C]
+                xh = x_blk[:, G * t + 2 * C : G * t + 3 * C]
+                hh = h_blk[:, C * t : C * t + C]
+
+                z = work.tile([P, C], F32)
+                r = work.tile([P, C], F32)
+                cnd = work.tile([P, C], F32)
+                u_t = work.tile([P, C], F32)
+                nc.gpsimd.tensor_tensor(out=z[:], in0=xz, in1=b_bc[:, 0:C], op=ALU.add)
+                nc.gpsimd.tensor_tensor(out=r[:], in0=xr, in1=b_bc[:, C : 2 * C], op=ALU.add)
+                nc.vector.tensor_tensor(out=r[:], in0=acc[1][:], in1=r[:], op=ALU.add)
+                nc.scalar.activation(out=r[:], in_=r[:], func=FN.Sigmoid)
+                nc.vector.tensor_tensor(out=z[:], in0=acc[0][:], in1=z[:], op=ALU.add)
+                nc.scalar.activation(out=z[:], in_=z[:], func=FN.Sigmoid)
+                nc.vector.tensor_tensor(out=cnd[:], in0=acc[2][:], in1=b_bc[:, 2 * C : 3 * C], op=ALU.add)
+                nc.vector.tensor_tensor(out=cnd[:], in0=cnd[:], in1=r[:], op=ALU.mult)
+                nc.vector.tensor_tensor(out=cnd[:], in0=cnd[:], in1=xh, op=ALU.add)
+                nc.scalar.activation(out=cnd[:], in_=cnd[:], func=FN.Tanh)
+                nc.vector.tensor_tensor(out=u_t[:], in0=hh, in1=cnd[:], op=ALU.subtract)
+                nc.vector.tensor_tensor(out=u_t[:], in0=u_t[:], in1=z[:], op=ALU.mult)
+                nc.vector.tensor_tensor(out=o_blk[:, C * t : C * t + C], in0=u_t[:], in1=cnd[:], op=ALU.add)
+            nc.sync.dma_start(out=out_all[rows, :].rearrange("(p t) c -> p (t c)", t=TPB), in_=o_blk[:])

@@ -16,6 +16,7 @@ C = 512
 G = 3 * C
 R = 4096
 TPB = 4
+NFC = C // P
 BLOCK = P * TPB
 NBLK = R // BLOCK
 
@@ -30,32 +31,65 @@ def tile_gatedgraphconvolution_pb_t_kernel(tc, x_proj, annotations, recurrent_ke
     with ExitStack() as ctx:
         const = ctx.enter_context(tc.tile_pool(name="const", bufs=1))
         xpool = ctx.enter_context(tc.tile_pool(name="xpool", bufs=3))
-        hpool = ctx.enter_context(tc.tile_pool(name="hpool", bufs=3))
+        hpool = ctx.enter_context(tc.tile_pool(name="hpool", bufs=4))
         qpool = ctx.enter_context(tc.tile_pool(name="qpool", bufs=2))
         work = ctx.enter_context(tc.tile_pool(name="work", bufs=4))
         opool = ctx.enter_context(tc.tile_pool(name="opool", bufs=3))
+        ps_n = ctx.enter_context(tc.psum_pool(name="ps_n", bufs=3))
         ps_t = ctx.enter_context(tc.psum_pool(name="ps_t", bufs=2))
-        ps_m = ctx.enter_context(tc.psum_pool(name="ps_m", bufs=6))
+        ps_c = ctx.enter_context(tc.psum_pool(name="ps_c", bufs=1))
+        ps_m = ctx.enter_context(tc.psum_pool(name="ps_m", bufs=1))
+        ps_z = ctx.enter_context(tc.psum_pool(name="ps_z", bufs=1))
 
         ident = const.tile([P, P], F32)
         make_identity(nc, ident[:])
 
+        def load_block(b):
+            rows = slice(BLOCK * b, BLOCK * b + BLOCK)
+            h_blk = hpool.tile([P, TPB * C], BF16, name="h_blk", tag="h_blk")
+            nc.sync.dma_start(out=h_blk[:], in_=h_all[rows, :].rearrange("(p t) c -> p (t c)", t=TPB))
+            return h_blk
+
+        def load_x(b):
+            rows = slice(BLOCK * b, BLOCK * b + BLOCK)
+            x_blk = xpool.tile([P, TPB * G], BF16, name="x_blk", tag="x_blk")
+            nc.sync.dma_start(out=x_blk[:], in_=x_proj[rows, :].rearrange("(p t) c -> p (t c)", t=TPB))
+            return x_blk
+
+        h_first = load_block(0)
+
         w_raw = const.tile([P, 4, G], BF16)
-        for u in range(2):
-            nc.sync.dma_start(
-                out=w_raw[:, 2 * u : 2 * u + 2, :],
-                in_=recurrent_kernel[256 * u : 256 * u + 256, :].rearrange("(q e) c -> q e c", e=2),
-            )
-        b_bc = const.tile([P, G], BF16)
-        nc.scalar.dma_start(out=b_bc[:], in_=bias_h.partition_broadcast(P))
+        gate_order = (1, 2, 0)
+        for g in gate_order:
+            cs = slice(C * g, C * g + C)
+            for u in range(2):
+                nc.sync.dma_start(
+                    out=w_raw[:, 2 * u : 2 * u + 2, cs],
+                    in_=recurrent_kernel[256 * u : 256 * u + 256, cs].rearrange("(q e) c -> q e c", e=2),
+                )
+        x_first = load_x(0)
+
+        b_rows = const.tile([P, P], BF16)
+        nc.gpsimd.memset(b_rows[:], 0.0)
+        nc.scalar.dma_start(out=b_rows[0 : G // P, :], in_=bias_h.rearrange("(j q) -> j q", q=P))
+        b_rows32 = const.tile([P, P], F32)
+        nc.vector.tensor_copy(out=b_rows32[:], in_=b_rows[:])
+        b_ps = ps_n.tile([P, C], F32, name="b_ps", tag="n")
+        nc.tensor.transpose(b_ps[:, 0:P], b_rows32[:], ident[:])
+        b_col = const.tile([P, G // P], F32)
+        nc.vector.tensor_copy(out=b_col[:], in_=b_ps[:, 0 : G // P])
 
         w_grp = const.tile([P, G, 4], BF16, align_bytes=64)
         w_codes = const.tile([P, G], U32, align_bytes=64)
         w_scales = const.tile([P, G], U8, align_bytes=64)
-        for g in range(3):
+        for g in gate_order:
             cs = slice(C * g, C * g + C)
-            nc.vector.tensor_copy(out=w_grp[:, cs, :], in_=w_raw[:, :, cs].rearrange("q t c -> q c t"))
-        for g in range(3):
+            if g == 0:
+                nc.scalar.copy(out=w_grp[:, cs, :], in_=w_raw[:, :, cs].rearrange("q t c -> q c t"))
+            else:
+                nc.vector.tensor_copy(out=w_grp[:, cs, :], in_=w_raw[:, :, cs].rearrange("q t c -> q c t"))
+
+        def quantise_w(g):
             cs = slice(C * g, C * g + C)
             nc.vector.quantize_mx(
                 out=w_codes[:, cs].bitcast(FP8X4),
@@ -63,18 +97,19 @@ def tile_gatedgraphconvolution_pb_t_kernel(tc, x_proj, annotations, recurrent_ke
                 in_=w_grp[:, cs, :].rearrange("q c t -> q (c t)"),
             )
 
+        for g in gate_order:
+            quantise_w(g)
+
         for b in range(NBLK):
             rows = slice(BLOCK * b, BLOCK * b + BLOCK)
-            h_blk = hpool.tile([P, TPB * C], BF16)
-            nc.sync.dma_start(out=h_blk[:], in_=h_all[rows, :].rearrange("(p t) c -> p (t c)", t=TPB))
-            x_blk = xpool.tile([P, TPB * G], BF16)
-            nc.sync.dma_start(out=x_blk[:], in_=x_proj[rows, :].rearrange("(p t) c -> p (t c)", t=TPB))
+            h_blk = h_first if b == 0 else load_block(b)
+            x_blk = x_first if b == 0 else load_x(b)
 
             h_words = h_blk[:].bitcast(F32)
             h_grp = qpool.tile([P, 4 * BLOCK], BF16, align_bytes=64)
             h_grp_w = h_grp[:].bitcast(F32).rearrange("q (t p u) -> q t p u", t=TPB, u=2)
             for half in range(2):
-                xt = ps_t.tile([P, 4, P], F32)
+                xt = ps_n.tile([P, 4, P], F32, name="xt", tag="n")
                 for j in range(4):
                     t = 2 * half + j // 2
                     u = j % 2
@@ -87,13 +122,12 @@ def tile_gatedgraphconvolution_pb_t_kernel(tc, x_proj, annotations, recurrent_ke
             h_scales = qpool.tile([P, BLOCK], U8, align_bytes=64)
             nc.vector.quantize_mx(out=h_codes[:].bitcast(FP8X4), scales=h_scales[:], in_=h_grp[:])
 
-            o_blk = opool.tile([P, TPB * C], F32)
-            for t in range(TPB):
-                ns = slice(P * t, P * t + P)
-                acc = []
-                for g in range(3):
+            def gate_nodes(g):
+                res = []
+                for t in range(TPB):
+                    ns = slice(P * t, P * t + P)
                     cs = slice(C * g, C * g + C)
-                    pg = ps_m.tile([P, C], F32, name="pg", tag="pg")
+                    pg = ps_n.tile([P, C], F32, name="pg", tag="n")
                     nc.tensor.matmul_mx(
                         out=pg[:],
                         lhsT=h_codes[:, ns].bitcast(FP8X4),
@@ -103,27 +137,75 @@ def tile_gatedgraphconvolution_pb_t_kernel(tc, x_proj, annotations, recurrent_ke
                         start=True,
                         stop=True,
                     )
-                    acc.append(pg)
-                xz = x_blk[:, G * t : G * t + C]
-                xr = x_blk[:, G * t + C : G * t + 2 * C]
-                xh = x_blk[:, G * t + 2 * C : G * t + 3 * C]
-                hh = h_blk[:, C * t : C * t + C]
+                    s = work.tile([P, C], F32, name="s", tag="ab", bufs=8)
+                    nc.vector.tensor_tensor(
+                        out=s[:], in0=pg[:], in1=x_blk[:, G * t + C * g : G * t + C * g + C], op=ALU.add
+                    )
+                    res.append(s)
+                return res
 
-                z = work.tile([P, C], F32)
-                r = work.tile([P, C], F32)
-                cnd = work.tile([P, C], F32)
-                u_t = work.tile([P, C], F32)
-                nc.gpsimd.tensor_tensor(out=z[:], in0=xz, in1=b_bc[:, 0:C], op=ALU.add)
-                nc.gpsimd.tensor_tensor(out=r[:], in0=xr, in1=b_bc[:, C : 2 * C], op=ALU.add)
-                nc.vector.tensor_tensor(out=r[:], in0=acc[1][:], in1=r[:], op=ALU.add)
-                nc.scalar.activation(out=r[:], in_=r[:], func=FN.Sigmoid)
-                nc.vector.tensor_tensor(out=z[:], in0=acc[0][:], in1=z[:], op=ALU.add)
-                nc.scalar.activation(out=z[:], in_=z[:], func=FN.Sigmoid)
-                nc.vector.tensor_tensor(out=cnd[:], in0=acc[2][:], in1=b_bc[:, 2 * C : 3 * C], op=ALU.add)
-                nc.vector.tensor_tensor(out=cnd[:], in0=cnd[:], in1=r[:], op=ALU.mult)
-                nc.vector.tensor_tensor(out=cnd[:], in0=cnd[:], in1=xh, op=ALU.add)
+            def flip(src, pool, tag):
+                def bank(j):
+                    ps = pool.tile([P, C], F32, name="ps_" + tag, tag=tag)
+                    for i in range(4):
+                        nc.tensor.transpose(ps[:, P * i : P * i + P], src[i][:, P * j : P * j + P], ident[:])
+                    return ps
+
+                return bank
+
+            def sigmoid_features(src, g, tag, bufs):
+                bank = flip(src, ps_t, "t")
+                res = []
+                for fc in range(NFC):
+                    ps = bank(fc)
+                    s = work.tile([P, C], F32, name="sg", tag=tag, bufs=bufs)
+                    nc.scalar.activation(
+                        out=s[:], in_=ps[:], func=FN.Sigmoid, bias=b_col[:, NFC * g + fc : NFC * g + fc + 1]
+                    )
+                    res.append(s)
+                return res
+
+            r_t = sigmoid_features(gate_nodes(1), 1, "rT", 5)
+
+            m_t = []
+            for fc in range(NFC):
+                cs = slice(2 * C + P * fc, 2 * C + P * fc + P)
+                pc = ps_c.tile([P, C], F32, name="pc", tag="c")
+                nc.tensor.matmul_mx(
+                    out=pc[:],
+                    lhsT=w_codes[:, cs].bitcast(FP8X4),
+                    lhsT_scale=w_scales[:, cs],
+                    rhs=h_codes[:].bitcast(FP8X4),
+                    rhs_scale=h_scales[:],
+                    start=True,
+                    stop=True,
+                )
+                m = work.tile([P, C], F32, name="m", tag="mT", bufs=5)
+                nc.vector.scalar_tensor_tensor(
+                    out=m[:],
+                    in0=pc[:],
+                    scalar=b_col[:, 2 * NFC + fc : 2 * NFC + fc + 1],
+                    in1=r_t[fc][:],
+                    op0=ALU.add,
+                    op1=ALU.mult,
+                )
+                m_t.append(m)
+
+            z_t = sigmoid_features(gate_nodes(0), 0, "zT", 9)
+
+            m_bank = flip(m_t, ps_m, "mn")
+            z_bank = flip(z_t, ps_z, "zn")
+            o_blk = opool.tile([P, TPB * C], F32)
+            for t in range(TPB):
+                mn = m_bank(t)
+                cnd = work.tile([P, C], F32, name="cnd", tag="cd", bufs=8)
+                nc.vector.tensor_tensor(
+                    out=cnd[:], in0=mn[:], in1=x_blk[:, G * t + 2 * C : G * t + 3 * C], op=ALU.add
+                )
                 nc.scalar.activation(out=cnd[:], in_=cnd[:], func=FN.Tanh)
-                nc.vector.tensor_tensor(out=u_t[:], in0=hh, in1=cnd[:], op=ALU.subtract)
-                nc.vector.tensor_tensor(out=u_t[:], in0=u_t[:], in1=z[:], op=ALU.mult)
-                nc.vector.tensor_tensor(out=o_blk[:, C * t : C * t + C], in0=u_t[:], in1=cnd[:], op=ALU.add)
+                u_t = work.tile([P, C], F32, name="u_t", tag="u", bufs=6)
+                nc.gpsimd.tensor_tensor(out=u_t[:], in0=h_blk[:, C * t : C * t + C], in1=cnd[:], op=ALU.subtract)
+                zn = z_bank(t)
+                nc.vector.tensor_tensor(out=u_t[:], in0=zn[:], in1=u_t[:], op=ALU.mult)
+                nc.gpsimd.tensor_tensor(out=o_blk[:, C * t : C * t + C], in0=u_t[:], in1=cnd[:], op=ALU.add)
             nc.sync.dma_start(out=out_all[rows, :].rearrange("(p t) c -> p (t c)", t=TPB), in_=o_blk[:])

@@ -22,6 +22,8 @@ NBLK = R // BLOCK
 
 FLOPS = 2 * R * C * G
 
+NT = R // P
+
 
 def tile_gatedgraphconvolution_pb_t_kernel(tc, x_proj, annotations, recurrent_kernel, bias_h, out):
     nc = tc.nc
@@ -29,65 +31,67 @@ def tile_gatedgraphconvolution_pb_t_kernel(tc, x_proj, annotations, recurrent_ke
     out_all = out.flatten_outer_dims()
 
     with ExitStack() as ctx:
+        ctx.enter_context(tc.manual_schedule())
         const = ctx.enter_context(tc.tile_pool(name="const", bufs=1))
         xpool = ctx.enter_context(tc.tile_pool(name="xpool", bufs=3))
-        hpool = ctx.enter_context(tc.tile_pool(name="hpool", bufs=4))
-        qpool = ctx.enter_context(tc.tile_pool(name="qpool", bufs=2))
-        work = ctx.enter_context(tc.tile_pool(name="work", bufs=4))
-        opool = ctx.enter_context(tc.tile_pool(name="opool", bufs=3))
-        ps_n = ctx.enter_context(tc.psum_pool(name="ps_n", bufs=3))
+        hpool = ctx.enter_context(tc.tile_pool(name="hpool", bufs=3))
+        qpool = ctx.enter_context(tc.tile_pool(name="qpool", bufs=3))
+        work = ctx.enter_context(tc.tile_pool(name="work", bufs=3))
+        opool = ctx.enter_context(tc.tile_pool(name="opool", bufs=2))
+        ps_x = ctx.enter_context(tc.psum_pool(name="ps_x", bufs=1))
+        ps_n = ctx.enter_context(tc.psum_pool(name="ps_n", bufs=2))
         ps_t = ctx.enter_context(tc.psum_pool(name="ps_t", bufs=2))
         ps_c = ctx.enter_context(tc.psum_pool(name="ps_c", bufs=1))
         ps_m = ctx.enter_context(tc.psum_pool(name="ps_m", bufs=1))
         ps_z = ctx.enter_context(tc.psum_pool(name="ps_z", bufs=1))
 
-        ident = const.tile([P, P], F32)
-        make_identity(nc, ident[:])
+        h_blks = {}
+        x_blks = {}
+        o_blks = {}
 
-        def load_block(b):
+        def load_h(b):
             rows = slice(BLOCK * b, BLOCK * b + BLOCK)
             h_blk = hpool.tile([P, TPB * C], BF16, name="h_blk", tag="h_blk")
             nc.sync.dma_start(out=h_blk[:], in_=h_all[rows, :].rearrange("(p t) c -> p (t c)", t=TPB))
-            return h_blk
+            h_blks[b] = h_blk
 
         def load_x(b):
             rows = slice(BLOCK * b, BLOCK * b + BLOCK)
             x_blk = xpool.tile([P, TPB * G], BF16, name="x_blk", tag="x_blk")
             nc.sync.dma_start(out=x_blk[:], in_=x_proj[rows, :].rearrange("(p t) c -> p (t c)", t=TPB))
-            return x_blk
+            x_blks[b] = x_blk
 
-        h_first = load_block(0)
+        ident = const.tile([P, P], F32)
+        make_identity(nc, ident[:])
+        b_rows = const.tile([P, P], BF16)
+        nc.gpsimd.memset(b_rows[:], 0.0)
+        nc.scalar.dma_start(out=b_rows[0 : G // P, :], in_=bias_h.rearrange("(j q) -> j q", q=P))
 
         w_raw = const.tile([P, 4, G], BF16)
         gate_order = (1, 2, 0)
-        for g in gate_order:
+
+        def load_w(g):
             cs = slice(C * g, C * g + C)
             for u in range(2):
                 nc.sync.dma_start(
                     out=w_raw[:, 2 * u : 2 * u + 2, cs],
                     in_=recurrent_kernel[256 * u : 256 * u + 256, cs].rearrange("(q e) c -> q e c", e=2),
                 )
-        x_first = load_x(0)
 
-        b_rows = const.tile([P, P], BF16)
-        nc.gpsimd.memset(b_rows[:], 0.0)
-        nc.scalar.dma_start(out=b_rows[0 : G // P, :], in_=bias_h.rearrange("(j q) -> j q", q=P))
-        b_rows32 = const.tile([P, P], F32)
-        nc.vector.tensor_copy(out=b_rows32[:], in_=b_rows[:])
-        b_ps = ps_n.tile([P, C], F32, name="b_ps", tag="n")
-        nc.tensor.transpose(b_ps[:, 0:P], b_rows32[:], ident[:])
-        b_col = const.tile([P, G // P], F32)
-        nc.vector.tensor_copy(out=b_col[:], in_=b_ps[:, 0 : G // P])
+        load_w(1)
+        load_h(0)
+        load_w(2)
+        load_w(0)
+        load_x(0)
+        load_h(1)
+        load_x(1)
 
         w_grp = const.tile([P, G, 4], BF16, align_bytes=64)
         w_codes = const.tile([P, G], U32, align_bytes=64)
         w_scales = const.tile([P, G], U8, align_bytes=64)
-        for g in gate_order:
-            cs = slice(C * g, C * g + C)
-            if g == 0:
-                nc.scalar.copy(out=w_grp[:, cs, :], in_=w_raw[:, :, cs].rearrange("q t c -> q c t"))
-            else:
-                nc.vector.tensor_copy(out=w_grp[:, cs, :], in_=w_raw[:, :, cs].rearrange("q t c -> q c t"))
+
+        def regroup_w(eng_copy, lo, hi):
+            eng_copy(out=w_grp[:, lo:hi, :], in_=w_raw[:, :, lo:hi].rearrange("q t c -> q c t"))
 
         def quantise_w(g):
             cs = slice(C * g, C * g + C)
@@ -97,115 +101,195 @@ def tile_gatedgraphconvolution_pb_t_kernel(tc, x_proj, annotations, recurrent_ke
                 in_=w_grp[:, cs, :].rearrange("q c t -> q (c t)"),
             )
 
-        for g in gate_order:
-            quantise_w(g)
+        st = {}
 
-        for b in range(NBLK):
-            rows = slice(BLOCK * b, BLOCK * b + BLOCK)
-            h_blk = h_first if b == 0 else load_block(b)
-            x_blk = x_first if b == 0 else load_x(b)
+        def ok(i):
+            return 0 <= i < NT
 
-            h_words = h_blk[:].bitcast(F32)
-            h_grp = qpool.tile([P, 4 * BLOCK], BF16, align_bytes=64)
-            h_grp_w = h_grp[:].bitcast(F32).rearrange("q (t p u) -> q t p u", t=TPB, u=2)
-            for half in range(2):
-                xt = ps_n.tile([P, 4, P], F32, name="xt", tag="n")
-                for j in range(4):
-                    t = 2 * half + j // 2
-                    u = j % 2
-                    nc.tensor.transpose(xt[:, j, :], h_words[:, 256 * t + P * u : 256 * t + P * u + P], ident[:])
-                nc.scalar.copy(
-                    out=h_grp_w[:, 2 * half : 2 * half + 2, :, :],
-                    in_=xt[:].rearrange("q (t u) p -> q t p u", u=2),
-                )
-            h_codes = qpool.tile([P, BLOCK], U32, align_bytes=64)
-            h_scales = qpool.tile([P, BLOCK], U8, align_bytes=64)
-            nc.vector.quantize_mx(out=h_codes[:].bitcast(FP8X4), scales=h_scales[:], in_=h_grp[:])
+        def x_of(i, g):
+            t = i % TPB
+            return x_blks[i // TPB][:, G * t + C * g : G * t + C * g + C]
 
-            def gate_nodes(g):
-                res = []
-                for t in range(TPB):
-                    ns = slice(P * t, P * t + P)
-                    cs = slice(C * g, C * g + C)
-                    pg = ps_n.tile([P, C], F32, name="pg", tag="n")
-                    nc.tensor.matmul_mx(
-                        out=pg[:],
-                        lhsT=h_codes[:, ns].bitcast(FP8X4),
-                        lhsT_scale=h_scales[:, ns],
-                        rhs=w_codes[:, cs].bitcast(FP8X4),
-                        rhs_scale=w_scales[:, cs],
-                        start=True,
-                        stop=True,
-                    )
-                    s = work.tile([P, C], F32, name="s", tag="ab", bufs=8)
-                    nc.vector.tensor_tensor(
-                        out=s[:], in0=pg[:], in1=x_blk[:, G * t + C * g : G * t + C * g + C], op=ALU.add
-                    )
-                    res.append(s)
-                return res
+        def s_ht(i):
+            t = i % TPB
+            h_words = h_blks[i // TPB][:].bitcast(F32)
+            xt = ps_x.tile([P, 2, P], F32, name="xt", tag="xt")
+            for u in range(2):
+                nc.tensor.transpose(xt[:, u, :], h_words[:, 256 * t + P * u : 256 * t + P * u + P], ident[:])
+            h_grp = qpool.tile([P, 4 * P], BF16, name="h_grp", tag="h_grp", align_bytes=64)
+            nc.scalar.copy(
+                out=h_grp[:].bitcast(F32).rearrange("q (p u) -> q p u", u=2),
+                in_=xt[:].rearrange("q u p -> q p u"),
+            )
+            st[("grp", i)] = h_grp
 
-            def flip(src, pool, tag):
-                def bank(j):
-                    ps = pool.tile([P, C], F32, name="ps_" + tag, tag=tag)
-                    for i in range(4):
-                        nc.tensor.transpose(ps[:, P * i : P * i + P], src[i][:, P * j : P * j + P], ident[:])
-                    return ps
+        def s_quant(i):
+            h_codes = qpool.tile([P, P], U32, name="h_codes", tag="h_codes", align_bytes=64)
+            h_scales = qpool.tile([P, P], U8, name="h_scales", tag="h_scales", align_bytes=64)
+            nc.vector.quantize_mx(out=h_codes[:].bitcast(FP8X4), scales=h_scales[:], in_=st[("grp", i)][:])
+            st[("hc", i)] = h_codes
+            st[("hs", i)] = h_scales
 
-                return bank
-
-            def sigmoid_features(src, g, tag, bufs):
-                bank = flip(src, ps_t, "t")
-                res = []
-                for fc in range(NFC):
-                    ps = bank(fc)
-                    s = work.tile([P, C], F32, name="sg", tag=tag, bufs=bufs)
-                    nc.scalar.activation(
-                        out=s[:], in_=ps[:], func=FN.Sigmoid, bias=b_col[:, NFC * g + fc : NFC * g + fc + 1]
-                    )
-                    res.append(s)
-                return res
-
-            r_t = sigmoid_features(gate_nodes(1), 1, "rT", 5)
-
-            m_t = []
-            for fc in range(NFC):
-                cs = slice(2 * C + P * fc, 2 * C + P * fc + P)
-                pc = ps_c.tile([P, C], F32, name="pc", tag="c")
+        def s_mx(i):
+            hc = st[("hc", i)]
+            hs = st[("hs", i)]
+            for g in (1, 0):
+                cs = slice(C * g, C * g + C)
+                pg = ps_n.tile([P, C], F32, name="pg", tag="n")
                 nc.tensor.matmul_mx(
-                    out=pc[:],
-                    lhsT=w_codes[:, cs].bitcast(FP8X4),
-                    lhsT_scale=w_scales[:, cs],
-                    rhs=h_codes[:].bitcast(FP8X4),
-                    rhs_scale=h_scales[:],
+                    out=pg[:],
+                    lhsT=hc[:].bitcast(FP8X4),
+                    lhsT_scale=hs[:],
+                    rhs=w_codes[:, cs].bitcast(FP8X4),
+                    rhs_scale=w_scales[:, cs],
                     start=True,
                     stop=True,
                 )
-                m = work.tile([P, C], F32, name="m", tag="mT", bufs=5)
+                st[("p", g, i)] = pg
+            pc = ps_c.tile([P, C], F32, name="pc", tag="c")
+            for fc in range(NFC):
+                cs = slice(2 * C + P * fc, 2 * C + P * fc + P)
+                nc.tensor.matmul_mx(
+                    out=pc[:, P * fc : P * fc + P],
+                    lhsT=w_codes[:, cs].bitcast(FP8X4),
+                    lhsT_scale=w_scales[:, cs],
+                    rhs=hc[:].bitcast(FP8X4),
+                    rhs_scale=hs[:],
+                    start=True,
+                    stop=True,
+                )
+            st[("pc", i)] = pc
+
+        def s_add_x(i, g):
+            s = work.tile([P, C], F32, name="s", tag="ab", bufs=4)
+            nc.vector.tensor_tensor(out=s[:], in0=st[("p", g, i)][:], in1=x_of(i, g), op=ALU.add)
+            st[("s", g, i)] = s
+
+        def flip(src, pool, tag):
+            ps = pool.tile([P, C], F32, name="ps_" + tag, tag=tag)
+            for j in range(4):
+                nc.tensor.transpose(ps[:, P * j : P * j + P], src[:, P * j : P * j + P], ident[:])
+            return ps
+
+        def s_flip_gate(i, g):
+            st[("sT", g, i)] = flip(st[("s", g, i)], ps_t, "t")
+
+        def s_sigmoid(i, g):
+            ps = st[("sT", g, i)]
+            s = work.tile([P, C], F32, name="sg", tag="sg%d" % g, bufs=(3 if g == 1 else 5))
+            for fc in range(NFC):
+                nc.scalar.activation(
+                    out=s[:, P * fc : P * fc + P],
+                    in_=ps[:, P * fc : P * fc + P],
+                    func=FN.Sigmoid,
+                    bias=b_col[:, NFC * g + fc : NFC * g + fc + 1],
+                )
+            st[("gT", g, i)] = s
+
+        def s_m(i):
+            m = work.tile([P, C], F32, name="m", tag="mT", bufs=3)
+            pc = st[("pc", i)]
+            r_t = st[("gT", 1, i)]
+            for fc in range(NFC):
+                fs = slice(P * fc, P * fc + P)
                 nc.vector.scalar_tensor_tensor(
-                    out=m[:],
-                    in0=pc[:],
+                    out=m[:, fs],
+                    in0=pc[:, fs],
                     scalar=b_col[:, 2 * NFC + fc : 2 * NFC + fc + 1],
-                    in1=r_t[fc][:],
+                    in1=r_t[:, fs],
                     op0=ALU.add,
                     op1=ALU.mult,
                 )
-                m_t.append(m)
+            st[("m", i)] = m
 
-            z_t = sigmoid_features(gate_nodes(0), 0, "zT", 9)
+        def s_flip_m(i):
+            st[("mn", i)] = flip(st[("m", i)], ps_m, "mn")
 
-            m_bank = flip(m_t, ps_m, "mn")
-            z_bank = flip(z_t, ps_z, "zn")
-            o_blk = opool.tile([P, TPB * C], F32)
-            for t in range(TPB):
-                mn = m_bank(t)
-                cnd = work.tile([P, C], F32, name="cnd", tag="cd", bufs=8)
-                nc.vector.tensor_tensor(
-                    out=cnd[:], in0=mn[:], in1=x_blk[:, G * t + 2 * C : G * t + 3 * C], op=ALU.add
-                )
-                nc.scalar.activation(out=cnd[:], in_=cnd[:], func=FN.Tanh)
-                u_t = work.tile([P, C], F32, name="u_t", tag="u", bufs=6)
-                nc.gpsimd.tensor_tensor(out=u_t[:], in0=h_blk[:, C * t : C * t + C], in1=cnd[:], op=ALU.subtract)
-                zn = z_bank(t)
-                nc.vector.tensor_tensor(out=u_t[:], in0=zn[:], in1=u_t[:], op=ALU.mult)
-                nc.gpsimd.tensor_tensor(out=o_blk[:, C * t : C * t + C], in0=u_t[:], in1=cnd[:], op=ALU.add)
-            nc.sync.dma_start(out=out_all[rows, :].rearrange("(p t) c -> p (t c)", t=TPB), in_=o_blk[:])
+        def s_ac(i):
+            cnd = work.tile([P, C], F32, name="cnd", tag="cd", bufs=5)
+            nc.vector.tensor_tensor(out=cnd[:], in0=st[("mn", i)][:], in1=x_of(i, 2), op=ALU.add)
+            st[("cd", i)] = cnd
+
+        def s_tanh(i):
+            cnd = st[("cd", i)]
+            nc.scalar.activation(out=cnd[:], in_=cnd[:], func=FN.Tanh)
+
+        def s_u(i):
+            t = i % TPB
+            u_t = work.tile([P, C], F32, name="u_t", tag="u", bufs=4)
+            nc.gpsimd.tensor_tensor(
+                out=u_t[:], in0=h_blks[i // TPB][:, C * t : C * t + C], in1=st[("cd", i)][:], op=ALU.subtract
+            )
+            st[("u", i)] = u_t
+
+        def s_flip_z(i):
+            st[("zn", i)] = flip(st[("gT", 0, i)], ps_z, "zn")
+
+        def s_v(i):
+            u_t = st[("u", i)]
+            nc.vector.tensor_tensor(out=u_t[:], in0=st[("zn", i)][:], in1=u_t[:], op=ALU.mult)
+
+        def s_out(i):
+            b = i // TPB
+            t = i % TPB
+            if t == 0:
+                o_blks[b] = opool.tile([P, TPB * C], F32, name="o_blk", tag="o_blk")
+            o_blk = o_blks[b]
+            nc.gpsimd.tensor_tensor(
+                out=o_blk[:, C * t : C * t + C], in0=st[("u", i)][:], in1=st[("cd", i)][:], op=ALU.add
+            )
+            dst = out_all[BLOCK * b : BLOCK * b + BLOCK, :].rearrange("(p t) c -> p t c", t=TPB)
+            if b == NBLK - 1:
+                nc.sync.dma_start(out=dst[:, t, :], in_=o_blk[:, C * t : C * t + C])
+            elif t == TPB - 1:
+                nc.sync.dma_start(out=dst, in_=o_blk[:].rearrange("p (t c) -> p t c", t=TPB))
+
+        for i in range(3):
+            s_ht(i)
+        regroup_w(nc.scalar.copy, 0, C // 2)
+        regroup_w(nc.vector.tensor_copy, C, 2 * C)
+        b_rows32 = const.tile([P, P], F32)
+        nc.vector.tensor_copy(out=b_rows32[:], in_=b_rows[:])
+        b_ps = ps_t.tile([P, C], F32, name="b_ps", tag="t")
+        nc.tensor.transpose(b_ps[:, 0:P], b_rows32[:], ident[:])
+        regroup_w(nc.vector.tensor_copy, 2 * C, 3 * C)
+        quantise_w(1)
+        s_quant(0)
+        regroup_w(nc.vector.tensor_copy, C // 2, C)
+        quantise_w(2)
+        b_col = const.tile([P, G // P], F32)
+        nc.vector.tensor_copy(out=b_col[:], in_=b_ps[:, 0 : G // P])
+        quantise_w(0)
+        s_mx(0)
+
+        for k in range(NT + 3):
+            if ok(k - 1):
+                s_flip_m(k - 1)
+            if ok(k):
+                s_add_x(k, 1)
+            if ok(k + 1):
+                s_quant(k + 1)
+            if ok(k):
+                s_flip_gate(k, 1)
+                s_sigmoid(k, 1)
+                s_add_x(k, 0)
+                s_flip_gate(k, 0)
+            if ok(k - 1):
+                s_ac(k - 1)
+                s_tanh(k - 1)
+            if ok(k):
+                s_m(k)
+                s_sigmoid(k, 0)
+            if ok(k - 1):
+                s_u(k - 1)
+            if ok(k - 2):
+                s_flip_z(k - 2)
+                s_v(k - 2)
+                s_out(k - 2)
+            if k % TPB == 1 and k // TPB + 2 < NBLK:
+                load_h(k // TPB + 2)
+                load_x(k // TPB + 2)
+            if ok(k + 3):
+                s_ht(k + 3)
+            if ok(k + 1):
+                s_mx(k + 1)

@@ -21,7 +21,6 @@ BLOCK = P * TPB
 NBLK = R // BLOCK
 
 FLOPS = 2 * R * C * G
-
 NT = R // P
 
 
@@ -34,41 +33,28 @@ def tile_gatedgraphconvolution_pb_t_kernel(tc, x_proj, annotations, recurrent_ke
         ctx.enter_context(tc.manual_schedule())
         const = ctx.enter_context(tc.tile_pool(name="const", bufs=1))
         xpool = ctx.enter_context(tc.tile_pool(name="xpool", bufs=3))
-        hpool = ctx.enter_context(tc.tile_pool(name="hpool", bufs=3))
+        hpool = ctx.enter_context(tc.tile_pool(name="hpool", bufs=4))
         qpool = ctx.enter_context(tc.tile_pool(name="qpool", bufs=3))
         work = ctx.enter_context(tc.tile_pool(name="work", bufs=3))
-        opool = ctx.enter_context(tc.tile_pool(name="opool", bufs=2))
-        ps_x = ctx.enter_context(tc.psum_pool(name="ps_x", bufs=1))
-        ps_n = ctx.enter_context(tc.psum_pool(name="ps_n", bufs=2))
-        ps_t = ctx.enter_context(tc.psum_pool(name="ps_t", bufs=2))
-        ps_c = ctx.enter_context(tc.psum_pool(name="ps_c", bufs=1))
-        ps_m = ctx.enter_context(tc.psum_pool(name="ps_m", bufs=1))
-        ps_z = ctx.enter_context(tc.psum_pool(name="ps_z", bufs=1))
+        opool = ctx.enter_context(tc.tile_pool(name="opool", bufs=3))
+        psum = ctx.enter_context(tc.psum_pool(name="psum", bufs=1))
 
         h_blks = {}
         x_blks = {}
         o_blks = {}
+        st = {}
 
         def load_h(b):
             rows = slice(BLOCK * b, BLOCK * b + BLOCK)
-            h_blk = hpool.tile([P, TPB * C], BF16, name="h_blk", tag="h_blk")
-            nc.sync.dma_start(out=h_blk[:], in_=h_all[rows, :].rearrange("(p t) c -> p (t c)", t=TPB))
-            h_blks[b] = h_blk
+            h_blks[b] = hpool.tile([P, TPB * C], BF16, name="h_blk", tag="h_blk")
+            nc.sync.dma_start(out=h_blks[b][:], in_=h_all[rows, :].rearrange("(p t) c -> p (t c)", t=TPB))
 
         def load_x(b):
-            rows = slice(BLOCK * b, BLOCK * b + BLOCK)
-            x_blk = xpool.tile([P, TPB * G], BF16, name="x_blk", tag="x_blk")
-            nc.sync.dma_start(out=x_blk[:], in_=x_proj[rows, :].rearrange("(p t) c -> p (t c)", t=TPB))
-            x_blks[b] = x_blk
-
-        ident = const.tile([P, P], F32)
-        make_identity(nc, ident[:])
-        b_rows = const.tile([P, P], BF16)
-        nc.gpsimd.memset(b_rows[:], 0.0)
-        nc.scalar.dma_start(out=b_rows[0 : G // P, :], in_=bias_h.rearrange("(j q) -> j q", q=P))
-
-        w_raw = const.tile([P, 4, G], BF16)
-        gate_order = (1, 2, 0)
+            src = x_proj[BLOCK * b : BLOCK * b + BLOCK, :].rearrange("(p t) c -> p t c", t=TPB)
+            x_blks[b] = xpool.tile([P, TPB, G], BF16, name="x_blk", tag="x_blk")
+            for half in range(2):
+                ts = slice(2 * half, 2 * half + 2)
+                nc.sync.dma_start(out=x_blks[b][:, ts, :], in_=src[:, ts, :])
 
         def load_w(g):
             cs = slice(C * g, C * g + C)
@@ -78,20 +64,9 @@ def tile_gatedgraphconvolution_pb_t_kernel(tc, x_proj, annotations, recurrent_ke
                     in_=recurrent_kernel[256 * u : 256 * u + 256, cs].rearrange("(q e) c -> q e c", e=2),
                 )
 
-        load_w(1)
-        load_h(0)
-        load_w(2)
-        load_w(0)
-        load_x(0)
-        load_h(1)
-        load_x(1)
-
-        w_grp = const.tile([P, G, 4], BF16, align_bytes=64)
-        w_codes = const.tile([P, G], U32, align_bytes=64)
-        w_scales = const.tile([P, G], U8, align_bytes=64)
-
-        def regroup_w(eng_copy, lo, hi):
-            eng_copy(out=w_grp[:, lo:hi, :], in_=w_raw[:, :, lo:hi].rearrange("q t c -> q c t"))
+        def regroup_w(g):
+            cs = slice(C * g, C * g + C)
+            nc.vector.tensor_copy(out=w_grp[:, cs, :], in_=w_raw[:, :, cs].rearrange("q t c -> q c t"))
 
         def quantise_w(g):
             cs = slice(C * g, C * g + C)
@@ -101,195 +76,217 @@ def tile_gatedgraphconvolution_pb_t_kernel(tc, x_proj, annotations, recurrent_ke
                 in_=w_grp[:, cs, :].rearrange("q c t -> q (c t)"),
             )
 
-        st = {}
-
-        def ok(i):
-            return 0 <= i < NT
-
         def x_of(i, g):
-            t = i % TPB
-            return x_blks[i // TPB][:, G * t + C * g : G * t + C * g + C]
+            return x_blks[i // TPB][:, i % TPB, C * g : C * g + C]
 
-        def s_ht(i):
+        def h_of(i):
             t = i % TPB
-            h_words = h_blks[i // TPB][:].bitcast(F32)
-            xt = ps_x.tile([P, 2, P], F32, name="xt", tag="xt")
+            return h_blks[i // TPB][:, C * t : C * t + C]
+
+        def flip(src, tag):
+            ps = psum.tile([P, C], F32, name="ps_" + tag, tag=tag)
+            for j in range(NFC):
+                nc.tensor.transpose(ps[:, P * j : P * j + P], src[:, P * j : P * j + P], ident[:])
+            return ps
+
+        def mx_nodes(i, g):
+            cs = slice(C * g, C * g + C)
+            pg = psum.tile([P, C], F32, name="pg", tag="p%d" % g)
+            nc.tensor.matmul_mx(
+                out=pg[:],
+                lhsT=st[("hc", i)][:].bitcast(FP8X4),
+                lhsT_scale=st[("hs", i)][:],
+                rhs=w_codes[:, cs].bitcast(FP8X4),
+                rhs_scale=w_scales[:, cs],
+                start=True,
+                stop=True,
+            )
+            st[("p", g, i)] = pg
+
+        def add_x(i, g):
+            s = work.tile([P, C], F32, name="s", tag="s%d" % g)
+            nc.vector.tensor_tensor(out=s[:], in0=st[("p", g, i)][:], in1=x_of(i, g), op=ALU.add)
+            st[("s", g, i)] = s
+
+        def sigmoid(i, g, bufs):
+            ps = st[("sT", g, i)]
+            s = work.tile([P, C], F32, name="sg", tag="sg%d" % g, bufs=bufs)
+            for fc in range(NFC):
+                fs = slice(P * fc, P * fc + P)
+                nc.scalar.activation(
+                    out=s[:, fs], in_=ps[:, fs], func=FN.Sigmoid, bias=b_col[:, NFC * g + fc : NFC * g + fc + 1]
+                )
+            st[("gT", g, i)] = s
+
+        def ht(i):
+            h_words = h_of(i).bitcast(F32)
+            xt = psum.tile([P, 2, P], F32, name="xt", tag="xt")
             for u in range(2):
-                nc.tensor.transpose(xt[:, u, :], h_words[:, 256 * t + P * u : 256 * t + P * u + P], ident[:])
+                nc.tensor.transpose(xt[:, u, :], h_words[:, P * u : P * u + P], ident[:])
+            st[("xt", i)] = xt
+
+        def ev(i):
             h_grp = qpool.tile([P, 4 * P], BF16, name="h_grp", tag="h_grp", align_bytes=64)
             nc.scalar.copy(
                 out=h_grp[:].bitcast(F32).rearrange("q (p u) -> q p u", u=2),
-                in_=xt[:].rearrange("q u p -> q p u"),
+                in_=st[("xt", i)][:].rearrange("q u p -> q p u"),
             )
             st[("grp", i)] = h_grp
 
-        def s_quant(i):
-            h_codes = qpool.tile([P, P], U32, name="h_codes", tag="h_codes", align_bytes=64)
-            h_scales = qpool.tile([P, P], U8, name="h_scales", tag="h_scales", align_bytes=64)
+        def q(i):
+            h_codes = qpool.tile([P, P], U32, name="h_codes", tag="h_codes", bufs=7, align_bytes=64)
+            h_scales = qpool.tile([P, P], U8, name="h_scales", tag="h_scales", bufs=7, align_bytes=64)
             nc.vector.quantize_mx(out=h_codes[:].bitcast(FP8X4), scales=h_scales[:], in_=st[("grp", i)][:])
             st[("hc", i)] = h_codes
             st[("hs", i)] = h_scales
 
-        def s_mx(i):
-            hc = st[("hc", i)]
-            hs = st[("hs", i)]
-            for g in (1, 0):
-                cs = slice(C * g, C * g + C)
-                pg = ps_n.tile([P, C], F32, name="pg", tag="n")
-                nc.tensor.matmul_mx(
-                    out=pg[:],
-                    lhsT=hc[:].bitcast(FP8X4),
-                    lhsT_scale=hs[:],
-                    rhs=w_codes[:, cs].bitcast(FP8X4),
-                    rhs_scale=w_scales[:, cs],
-                    start=True,
-                    stop=True,
-                )
-                st[("p", g, i)] = pg
-            pc = ps_c.tile([P, C], F32, name="pc", tag="c")
+        def mxr(i):
+            mx_nodes(i, 1)
+
+        def mxz(i):
+            mx_nodes(i, 0)
+
+        def mxc(i):
+            pc = psum.tile([P, C], F32, name="pc", tag="pc")
             for fc in range(NFC):
                 cs = slice(2 * C + P * fc, 2 * C + P * fc + P)
                 nc.tensor.matmul_mx(
                     out=pc[:, P * fc : P * fc + P],
                     lhsT=w_codes[:, cs].bitcast(FP8X4),
                     lhsT_scale=w_scales[:, cs],
-                    rhs=hc[:].bitcast(FP8X4),
-                    rhs_scale=hs[:],
+                    rhs=st[("hc", i)][:].bitcast(FP8X4),
+                    rhs_scale=st[("hs", i)][:],
                     start=True,
                     stop=True,
                 )
             st[("pc", i)] = pc
 
-        def s_add_x(i, g):
-            s = work.tile([P, C], F32, name="s", tag="ab", bufs=4)
-            nc.vector.tensor_tensor(out=s[:], in0=st[("p", g, i)][:], in1=x_of(i, g), op=ALU.add)
-            st[("s", g, i)] = s
+        def b0(i):
+            add_x(i, 1)
 
-        def flip(src, pool, tag):
-            ps = pool.tile([P, C], F32, name="ps_" + tag, tag=tag)
-            for j in range(4):
-                nc.tensor.transpose(ps[:, P * j : P * j + P], src[:, P * j : P * j + P], ident[:])
-            return ps
+        def a0(i):
+            add_x(i, 0)
 
-        def s_flip_gate(i, g):
-            st[("sT", g, i)] = flip(st[("s", g, i)], ps_t, "t")
+        def tb(i):
+            st[("sT", 1, i)] = flip(st[("s", 1, i)], "bt")
 
-        def s_sigmoid(i, g):
-            ps = st[("sT", g, i)]
-            s = work.tile([P, C], F32, name="sg", tag="sg%d" % g, bufs=(3 if g == 1 else 5))
-            for fc in range(NFC):
-                nc.scalar.activation(
-                    out=s[:, P * fc : P * fc + P],
-                    in_=ps[:, P * fc : P * fc + P],
-                    func=FN.Sigmoid,
-                    bias=b_col[:, NFC * g + fc : NFC * g + fc + 1],
-                )
-            st[("gT", g, i)] = s
+        def ta(i):
+            st[("sT", 0, i)] = flip(st[("s", 0, i)], "at")
 
-        def s_m(i):
-            m = work.tile([P, C], F32, name="m", tag="mT", bufs=3)
-            pc = st[("pc", i)]
-            r_t = st[("gT", 1, i)]
+        def sr(i):
+            sigmoid(i, 1, 3)
+
+        def sz(i):
+            sigmoid(i, 0, 4)
+
+        def m(i):
+            m_t = work.tile([P, C], F32, name="m_t", tag="mT")
             for fc in range(NFC):
                 fs = slice(P * fc, P * fc + P)
                 nc.vector.scalar_tensor_tensor(
-                    out=m[:, fs],
-                    in0=pc[:, fs],
+                    out=m_t[:, fs],
+                    in0=st[("pc", i)][:, fs],
                     scalar=b_col[:, 2 * NFC + fc : 2 * NFC + fc + 1],
-                    in1=r_t[:, fs],
+                    in1=st[("gT", 1, i)][:, fs],
                     op0=ALU.add,
                     op1=ALU.mult,
                 )
-            st[("m", i)] = m
+            st[("m", i)] = m_t
 
-        def s_flip_m(i):
-            st[("mn", i)] = flip(st[("m", i)], ps_m, "mn")
+        def tm(i):
+            st[("mn", i)] = flip(st[("m", i)], "mn")
 
-        def s_ac(i):
+        def ac(i):
             cnd = work.tile([P, C], F32, name="cnd", tag="cd", bufs=5)
             nc.vector.tensor_tensor(out=cnd[:], in0=st[("mn", i)][:], in1=x_of(i, 2), op=ALU.add)
             st[("cd", i)] = cnd
 
-        def s_tanh(i):
-            cnd = st[("cd", i)]
-            nc.scalar.activation(out=cnd[:], in_=cnd[:], func=FN.Tanh)
+        def th(i):
+            nc.scalar.activation(out=st[("cd", i)][:], in_=st[("cd", i)][:], func=FN.Tanh)
 
-        def s_u(i):
-            t = i % TPB
+        def u(i):
             u_t = work.tile([P, C], F32, name="u_t", tag="u", bufs=4)
-            nc.gpsimd.tensor_tensor(
-                out=u_t[:], in0=h_blks[i // TPB][:, C * t : C * t + C], in1=st[("cd", i)][:], op=ALU.subtract
-            )
+            nc.gpsimd.tensor_tensor(out=u_t[:], in0=h_of(i), in1=st[("cd", i)][:], op=ALU.subtract)
             st[("u", i)] = u_t
 
-        def s_flip_z(i):
-            st[("zn", i)] = flip(st[("gT", 0, i)], ps_z, "zn")
+        def tz(i):
+            st[("zn", i)] = flip(st[("gT", 0, i)], "zn")
 
-        def s_v(i):
-            u_t = st[("u", i)]
-            nc.vector.tensor_tensor(out=u_t[:], in0=st[("zn", i)][:], in1=u_t[:], op=ALU.mult)
+        def v(i):
+            nc.vector.tensor_tensor(out=st[("u", i)][:], in0=st[("zn", i)][:], in1=st[("u", i)][:], op=ALU.mult)
 
-        def s_out(i):
+        def o(i):
             b = i // TPB
             t = i % TPB
             if t == 0:
-                o_blks[b] = opool.tile([P, TPB * C], F32, name="o_blk", tag="o_blk")
-            o_blk = o_blks[b]
-            nc.gpsimd.tensor_tensor(
-                out=o_blk[:, C * t : C * t + C], in0=st[("u", i)][:], in1=st[("cd", i)][:], op=ALU.add
-            )
+                o_blks[b] = opool.tile([P, TPB, C], F32, name="o_blk", tag="o_blk")
+            nc.gpsimd.tensor_tensor(out=o_blks[b][:, t, :], in0=st[("u", i)][:], in1=st[("cd", i)][:], op=ALU.add)
             dst = out_all[BLOCK * b : BLOCK * b + BLOCK, :].rearrange("(p t) c -> p t c", t=TPB)
             if b == NBLK - 1:
-                nc.sync.dma_start(out=dst[:, t, :], in_=o_blk[:, C * t : C * t + C])
+                nc.sync.dma_start(out=dst[:, t, :], in_=o_blks[b][:, t, :])
             elif t == TPB - 1:
-                nc.sync.dma_start(out=dst, in_=o_blk[:].rearrange("p (t c) -> p t c", t=TPB))
+                nc.sync.dma_start(out=dst, in_=o_blks[b][:])
 
-        for i in range(3):
-            s_ht(i)
-        regroup_w(nc.scalar.copy, 0, C // 2)
-        regroup_w(nc.vector.tensor_copy, C, 2 * C)
+        def run(stage, i):
+            if 0 <= i < NT:
+                stage(i)
+
+        ident = const.tile([P, P], F32)
+        make_identity(nc, ident[:])
+        b_rows = const.tile([P, P], BF16)
+        nc.gpsimd.memset(b_rows[:], 0.0)
+        nc.scalar.dma_start(out=b_rows[0 : G // P, :], in_=bias_h.rearrange("(j q) -> j q", q=P))
+        w_raw = const.tile([P, 4, G], BF16)
+        w_grp = const.tile([P, G, 4], BF16, align_bytes=64)
+        w_codes = const.tile([P, G], U32, align_bytes=64)
+        w_scales = const.tile([P, G], U8, align_bytes=64)
+        load_w(1)
+        load_h(0)
+        load_x(0)
+        load_w(2)
+        load_w(0)
+        load_h(1)
+        load_x(1)
+
+        regroup_w(1)
         b_rows32 = const.tile([P, P], F32)
         nc.vector.tensor_copy(out=b_rows32[:], in_=b_rows[:])
-        b_ps = ps_t.tile([P, C], F32, name="b_ps", tag="t")
+        b_ps = psum.tile([P, C], F32, name="b_ps", tag="bt")
         nc.tensor.transpose(b_ps[:, 0:P], b_rows32[:], ident[:])
-        regroup_w(nc.vector.tensor_copy, 2 * C, 3 * C)
         quantise_w(1)
-        s_quant(0)
-        regroup_w(nc.vector.tensor_copy, C // 2, C)
-        quantise_w(2)
         b_col = const.tile([P, G // P], F32)
         nc.vector.tensor_copy(out=b_col[:], in_=b_ps[:, 0 : G // P])
-        quantise_w(0)
-        s_mx(0)
 
-        for k in range(NT + 3):
-            if ok(k - 1):
-                s_flip_m(k - 1)
-            if ok(k):
-                s_add_x(k, 1)
-            if ok(k + 1):
-                s_quant(k + 1)
-            if ok(k):
-                s_flip_gate(k, 1)
-                s_sigmoid(k, 1)
-                s_add_x(k, 0)
-                s_flip_gate(k, 0)
-            if ok(k - 1):
-                s_ac(k - 1)
-                s_tanh(k - 1)
-            if ok(k):
-                s_m(k)
-                s_sigmoid(k, 0)
-            if ok(k - 1):
-                s_u(k - 1)
-            if ok(k - 2):
-                s_flip_z(k - 2)
-                s_v(k - 2)
-                s_out(k - 2)
-            if k % TPB == 1 and k // TPB + 2 < NBLK:
-                load_h(k // TPB + 2)
-                load_x(k // TPB + 2)
-            if ok(k + 3):
-                s_ht(k + 3)
-            if ok(k + 1):
-                s_mx(k + 1)
+        for k in range(-4, NT + 6):
+            if k == -2:
+                regroup_w(2)
+            if k == -1:
+                regroup_w(0)
+            run(ac, k - 3)
+            run(mxz, k - 2)
+            run(b0, k)
+            run(mxc, k - 1)
+            run(ta, k - 3)
+            run(tz, k - 4)
+            run(ht, k + 4)
+            run(u, k - 4)
+            run(a0, k - 2)
+            run(sr, k - 1)
+            run(th, k - 3)
+            run(tm, k - 2)
+            run(m, k - 1)
+            run(o, k - 5)
+            run(v, k - 4)
+            run(tb, k)
+            run(sz, k - 3)
+            run(mxr, k + 2)
+            run(ev, k + 4)
+            run(q, k + 3)
+            if k == -2:
+                quantise_w(2)
+            if k == -1:
+                quantise_w(0)
+            if (k + 9) % TPB == 0 and 2 <= (k + 9) // TPB < NBLK:
+                load_h((k + 9) // TPB)
+            if (k + 6) % TPB == 0 and 2 <= (k + 6) // TPB < NBLK:
+                load_x((k + 6) // TPB)

@@ -34,8 +34,8 @@ def tile_gatedgraphconvolution_pb_t_kernel(tc, x_proj, annotations, recurrent_ke
         const = ctx.enter_context(tc.tile_pool(name="const", bufs=1))
         xpool = ctx.enter_context(tc.tile_pool(name="xpool", bufs=3))
         hpool = ctx.enter_context(tc.tile_pool(name="hpool", bufs=4))
-        qpool = ctx.enter_context(tc.tile_pool(name="qpool", bufs=3))
-        work = ctx.enter_context(tc.tile_pool(name="work", bufs=3))
+        qpool = ctx.enter_context(tc.tile_pool(name="qpool", bufs=4))
+        work = ctx.enter_context(tc.tile_pool(name="work", bufs=4))
         opool = ctx.enter_context(tc.tile_pool(name="opool", bufs=3))
         psum = ctx.enter_context(tc.psum_pool(name="psum", bufs=1))
 
@@ -64,9 +64,9 @@ def tile_gatedgraphconvolution_pb_t_kernel(tc, x_proj, annotations, recurrent_ke
                     in_=recurrent_kernel[256 * u : 256 * u + 256, cs].rearrange("(q e) c -> q e c", e=2),
                 )
 
-        def regroup_w(g):
+        def regroup_w(g, copy):
             cs = slice(C * g, C * g + C)
-            nc.vector.tensor_copy(out=w_grp[:, cs, :], in_=w_raw[:, :, cs].rearrange("q t c -> q c t"))
+            copy(out=w_grp[:, cs, :], in_=w_raw[:, :, cs].rearrange("q t c -> q c t"))
 
         def quantise_w(g):
             cs = slice(C * g, C * g + C)
@@ -134,8 +134,8 @@ def tile_gatedgraphconvolution_pb_t_kernel(tc, x_proj, annotations, recurrent_ke
             st[("grp", i)] = h_grp
 
         def q(i):
-            h_codes = qpool.tile([P, P], U32, name="h_codes", tag="h_codes", bufs=7, align_bytes=64)
-            h_scales = qpool.tile([P, P], U8, name="h_scales", tag="h_scales", bufs=7, align_bytes=64)
+            h_codes = qpool.tile([P, P], U32, name="h_codes", tag="h_codes", bufs=8, align_bytes=64)
+            h_scales = qpool.tile([P, P], U8, name="h_scales", tag="h_scales", bufs=8, align_bytes=64)
             nc.vector.quantize_mx(out=h_codes[:].bitcast(FP8X4), scales=h_scales[:], in_=st[("grp", i)][:])
             st[("hc", i)] = h_codes
             st[("hs", i)] = h_scales
@@ -174,10 +174,10 @@ def tile_gatedgraphconvolution_pb_t_kernel(tc, x_proj, annotations, recurrent_ke
             st[("sT", 0, i)] = flip(st[("s", 0, i)], "at")
 
         def sr(i):
-            sigmoid(i, 1, 3)
+            sigmoid(i, 1, 4)
 
         def sz(i):
-            sigmoid(i, 0, 4)
+            sigmoid(i, 0, 6)
 
         def m(i):
             m_t = work.tile([P, C], F32, name="m_t", tag="mT")
@@ -194,19 +194,31 @@ def tile_gatedgraphconvolution_pb_t_kernel(tc, x_proj, annotations, recurrent_ke
             st[("m", i)] = m_t
 
         def tm(i):
-            st[("mn", i)] = flip(st[("m", i)], "mn")
-
-        def ac(i):
-            cnd = work.tile([P, C], F32, name="cnd", tag="cd", bufs=5)
-            nc.vector.tensor_tensor(out=cnd[:], in0=st[("mn", i)][:], in1=x_of(i, 2), op=ALU.add)
-            st[("cd", i)] = cnd
+            mn = psum.tile([P, C], F32, name="mn", tag="mn")
+            nc.tensor.matmul(out=mn[:], lhsT=ident_bf[:], rhs=x_of(i, 2), start=True, stop=False)
+            for j in range(NFC):
+                js = slice(P * j, P * j + P)
+                nc.tensor.matmul(
+                    out=mn[:, js],
+                    lhsT=st[("m", i)][:, js],
+                    rhs=ident[:],
+                    is_transpose=True,
+                    start=False,
+                    stop=(j == NFC - 1),
+                )
+            st[("mn", i)] = mn
 
         def th(i):
-            nc.scalar.activation(out=st[("cd", i)][:], in_=st[("cd", i)][:], func=FN.Tanh)
+            cnd = work.tile([P, C], F32, name="cnd", tag="cd", bufs=6)
+            nc.scalar.activation(out=cnd[:], in_=st[("mn", i)][:], func=FN.Tanh)
+            st[("cd", i)] = cnd
+
+        def mix_engine(i):
+            return nc.vector if i >= NT - 2 else nc.gpsimd
 
         def u(i):
-            u_t = work.tile([P, C], F32, name="u_t", tag="u", bufs=4)
-            nc.gpsimd.tensor_tensor(out=u_t[:], in0=h_of(i), in1=st[("cd", i)][:], op=ALU.subtract)
+            u_t = work.tile([P, C], F32, name="u_t", tag="u", bufs=5)
+            mix_engine(i).tensor_tensor(out=u_t[:], in0=h_of(i), in1=st[("cd", i)][:], op=ALU.subtract)
             st[("u", i)] = u_t
 
         def tz(i):
@@ -220,7 +232,7 @@ def tile_gatedgraphconvolution_pb_t_kernel(tc, x_proj, annotations, recurrent_ke
             t = i % TPB
             if t == 0:
                 o_blks[b] = opool.tile([P, TPB, C], F32, name="o_blk", tag="o_blk")
-            nc.gpsimd.tensor_tensor(out=o_blks[b][:, t, :], in0=st[("u", i)][:], in1=st[("cd", i)][:], op=ALU.add)
+            mix_engine(i).tensor_tensor(out=o_blks[b][:, t, :], in0=st[("u", i)][:], in1=st[("cd", i)][:], op=ALU.add)
             dst = out_all[BLOCK * b : BLOCK * b + BLOCK, :].rearrange("(p t) c -> p t c", t=TPB)
             if b == NBLK - 1:
                 nc.sync.dma_start(out=dst[:, t, :], in_=o_blks[b][:, t, :])
@@ -233,6 +245,8 @@ def tile_gatedgraphconvolution_pb_t_kernel(tc, x_proj, annotations, recurrent_ke
 
         ident = const.tile([P, P], F32)
         make_identity(nc, ident[:])
+        ident_bf = const.tile([P, P], BF16)
+        make_identity(nc, ident_bf[:])
         b_rows = const.tile([P, P], BF16)
         nc.gpsimd.memset(b_rows[:], 0.0)
         nc.scalar.dma_start(out=b_rows[0 : G // P, :], in_=bias_h.rearrange("(j q) -> j q", q=P))
@@ -242,51 +256,47 @@ def tile_gatedgraphconvolution_pb_t_kernel(tc, x_proj, annotations, recurrent_ke
         w_scales = const.tile([P, G], U8, align_bytes=64)
         load_w(1)
         load_h(0)
-        load_x(0)
         load_w(2)
         load_w(0)
+        load_x(0)
         load_h(1)
         load_x(1)
-
-        regroup_w(1)
-        b_rows32 = const.tile([P, P], F32)
-        nc.vector.tensor_copy(out=b_rows32[:], in_=b_rows[:])
-        b_ps = psum.tile([P, C], F32, name="b_ps", tag="bt")
-        nc.tensor.transpose(b_ps[:, 0:P], b_rows32[:], ident[:])
+        regroup_w(1, nc.vector.tensor_copy)
         quantise_w(1)
+        b_rows32 = const.tile([P, P], F32)
         b_col = const.tile([P, G // P], F32)
-        nc.vector.tensor_copy(out=b_col[:], in_=b_ps[:, 0 : G // P])
 
-        for k in range(-4, NT + 6):
-            if k == -2:
-                regroup_w(2)
-            if k == -1:
-                regroup_w(0)
-            run(ac, k - 3)
-            run(mxz, k - 2)
-            run(b0, k)
-            run(mxc, k - 1)
-            run(ta, k - 3)
-            run(tz, k - 4)
-            run(ht, k + 4)
-            run(u, k - 4)
-            run(a0, k - 2)
-            run(sr, k - 1)
-            run(th, k - 3)
-            run(tm, k - 2)
-            run(m, k - 1)
-            run(o, k - 5)
-            run(v, k - 4)
-            run(tb, k)
-            run(sz, k - 3)
-            run(mxr, k + 2)
-            run(ev, k + 4)
-            run(q, k + 3)
-            if k == -2:
-                quantise_w(2)
+        for k in range(-3, NT + 5):
             if k == -1:
                 quantise_w(0)
-            if (k + 9) % TPB == 0 and 2 <= (k + 9) // TPB < NBLK:
-                load_h((k + 9) // TPB)
-            if (k + 6) % TPB == 0 and 2 <= (k + 6) // TPB < NBLK:
-                load_x((k + 6) // TPB)
+                nc.vector.tensor_copy(out=b_rows32[:], in_=b_rows[:])
+                quantise_w(2)
+                b_ps = psum.tile([P, C], F32, name="b_ps", tag="bt")
+                nc.tensor.transpose(b_ps[:, 0:P], b_rows32[:], ident[:])
+            if k == 0:
+                nc.vector.tensor_copy(out=b_col[:], in_=b_ps[:, 0 : G // P])
+            run(ev, k + 2)
+            run(v, k - 4)
+            run(sr, k - 1)
+            run(tm, k - 2)
+            run(tz, k - 3)
+            run(ta, k - 1)
+            run(ht, k + 3)
+            run(th, k - 2)
+            run(u, k - 3)
+            run(b0, k)
+            run(tb, k)
+            run(m, k - 1)
+            run(sz, k - 1)
+            run(a0, k)
+            run(mxr, k + 1)
+            run(mxc, k)
+            run(q, k + 2)
+            if k == -2:
+                regroup_w(2, nc.scalar.copy)
+                regroup_w(0, nc.vector.tensor_copy)
+            run(mxz, k + 1)
+            run(o, k - 4)
+            if (k + 7) % TPB == 0 and 2 <= (k + 7) // TPB < NBLK:
+                load_h((k + 7) // TPB)
+                load_x((k + 7) // TPB)

@@ -7,6 +7,7 @@ F32 = mybir.dt.float32
 BF16 = mybir.dt.bfloat16
 U32 = mybir.dt.uint32
 U8 = mybir.dt.uint8
+I32 = mybir.dt.int32
 FP8X4 = mybir.dt.float8_e4m3fn_x4
 ALU = mybir.AluOpType
 FN = mybir.ActivationFunctionType
@@ -193,7 +194,13 @@ def tile_gatedgraphconvolution_pb_t_kernel(tc, x_proj, annotations, recurrent_ke
                 )
             st[("m", i)] = m_t
 
+        def vector_adds_x(i):
+            return i % 3 != 0
+
         def tm(i):
+            if vector_adds_x(i):
+                st[("mn", i)] = flip(st[("m", i)], "mn")
+                return
             mn = psum.tile([P, C], F32, name="mn", tag="mn")
             nc.tensor.matmul(out=mn[:], lhsT=ident_bf[:], rhs=x_of(i, 2), start=True, stop=False)
             for j in range(NFC):
@@ -208,10 +215,14 @@ def tile_gatedgraphconvolution_pb_t_kernel(tc, x_proj, annotations, recurrent_ke
                 )
             st[("mn", i)] = mn
 
+        def ac(i):
+            st[("cd", i)] = work.tile([P, C], F32, name="cnd", tag="cd", bufs=6)
+            if vector_adds_x(i):
+                nc.vector.tensor_tensor(out=st[("cd", i)][:], in0=st[("mn", i)][:], in1=x_of(i, 2), op=ALU.add)
+
         def th(i):
-            cnd = work.tile([P, C], F32, name="cnd", tag="cd", bufs=6)
-            nc.scalar.activation(out=cnd[:], in_=st[("mn", i)][:], func=FN.Tanh)
-            st[("cd", i)] = cnd
+            src = st[("cd", i)] if vector_adds_x(i) else st[("mn", i)]
+            nc.scalar.activation(out=st[("cd", i)][:], in_=src[:], func=FN.Tanh)
 
         def mix_engine(i):
             return nc.vector if i >= NT - 2 else nc.gpsimd
@@ -243,13 +254,13 @@ def tile_gatedgraphconvolution_pb_t_kernel(tc, x_proj, annotations, recurrent_ke
             if 0 <= i < NT:
                 stage(i)
 
+        b_rows = const.tile([P, P], BF16)
+        nc.vector.memset(b_rows[:].bitcast(I32), 0)
+        nc.scalar.dma_start(out=b_rows[0 : G // P, :], in_=bias_h.rearrange("(j q) -> j q", q=P))
         ident = const.tile([P, P], F32)
         make_identity(nc, ident[:])
         ident_bf = const.tile([P, P], BF16)
         make_identity(nc, ident_bf[:])
-        b_rows = const.tile([P, P], BF16)
-        nc.gpsimd.memset(b_rows[:], 0.0)
-        nc.scalar.dma_start(out=b_rows[0 : G // P, :], in_=bias_h.rearrange("(j q) -> j q", q=P))
         w_raw = const.tile([P, 4, G], BF16)
         w_grp = const.tile([P, G, 4], BF16, align_bytes=64)
         w_codes = const.tile([P, G], U32, align_bytes=64)
@@ -262,41 +273,43 @@ def tile_gatedgraphconvolution_pb_t_kernel(tc, x_proj, annotations, recurrent_ke
         load_h(1)
         load_x(1)
         regroup_w(1, nc.vector.tensor_copy)
-        quantise_w(1)
+        regroup_w(2, nc.vector.tensor_copy)
         b_rows32 = const.tile([P, P], F32)
         b_col = const.tile([P, G // P], F32)
 
         for k in range(-3, NT + 5):
+            run(v, k - 4)
+            run(mxz, k)
+            run(u, k - 3)
+            run(mxr, k + 1)
+            run(sr, k - 1)
+            run(ht, k + 3)
+            run(tz, k - 3)
+            if k == -3:
+                quantise_w(1)
+            run(ac, k - 2)
+            run(q, k + 2)
+            if k == -2:
+                regroup_w(0, nc.vector.tensor_copy)
+            run(ta, k - 1)
+            run(m, k - 1)
+            if k == 0:
+                quantise_w(2)
+                nc.vector.tensor_copy(out=b_col[:], in_=b_ps[:, 0 : G // P])
+            run(tb, k)
+            run(th, k - 2)
+            run(a0, k)
+            run(ev, k + 3)
             if k == -1:
                 quantise_w(0)
                 nc.vector.tensor_copy(out=b_rows32[:], in_=b_rows[:])
-                quantise_w(2)
                 b_ps = psum.tile([P, C], F32, name="b_ps", tag="bt")
                 nc.tensor.transpose(b_ps[:, 0:P], b_rows32[:], ident[:])
-            if k == 0:
-                nc.vector.tensor_copy(out=b_col[:], in_=b_ps[:, 0 : G // P])
-            run(ev, k + 2)
-            run(v, k - 4)
-            run(sr, k - 1)
-            run(tm, k - 2)
-            run(tz, k - 3)
-            run(ta, k - 1)
-            run(ht, k + 3)
-            run(th, k - 2)
-            run(u, k - 3)
-            run(b0, k)
-            run(tb, k)
-            run(m, k - 1)
+            run(o, k - 5)
             run(sz, k - 1)
-            run(a0, k)
-            run(mxr, k + 1)
+            run(b0, k + 1)
+            run(tm, k - 1)
             run(mxc, k)
-            run(q, k + 2)
-            if k == -2:
-                regroup_w(2, nc.scalar.copy)
-                regroup_w(0, nc.vector.tensor_copy)
-            run(mxz, k + 1)
-            run(o, k - 4)
             if (k + 7) % TPB == 0 and 2 <= (k + 7) // TPB < NBLK:
                 load_h((k + 7) // TPB)
                 load_x((k + 7) // TPB)

@@ -128,7 +128,7 @@ def tile_gatedgraphconvolution_pb_t_kernel(tc, x_proj, annotations, recurrent_ke
 
         def ev(i):
             h_grp = qpool.tile([P, 4 * P], BF16, name="h_grp", tag="h_grp", align_bytes=64)
-            nc.scalar.copy(
+            nc.vector.tensor_copy(
                 out=h_grp[:].bitcast(F32).rearrange("q (p u) -> q p u", u=2),
                 in_=st[("xt", i)][:].rearrange("q u p -> q p u"),
             )
@@ -194,13 +194,7 @@ def tile_gatedgraphconvolution_pb_t_kernel(tc, x_proj, annotations, recurrent_ke
                 )
             st[("m", i)] = m_t
 
-        def vector_adds_x(i):
-            return i % 3 != 0
-
         def tm(i):
-            if vector_adds_x(i):
-                st[("mn", i)] = flip(st[("m", i)], "mn")
-                return
             mn = psum.tile([P, C], F32, name="mn", tag="mn")
             nc.tensor.matmul(out=mn[:], lhsT=ident_bf[:], rhs=x_of(i, 2), start=True, stop=False)
             for j in range(NFC):
@@ -215,14 +209,10 @@ def tile_gatedgraphconvolution_pb_t_kernel(tc, x_proj, annotations, recurrent_ke
                 )
             st[("mn", i)] = mn
 
-        def ac(i):
-            st[("cd", i)] = work.tile([P, C], F32, name="cnd", tag="cd", bufs=6)
-            if vector_adds_x(i):
-                nc.vector.tensor_tensor(out=st[("cd", i)][:], in0=st[("mn", i)][:], in1=x_of(i, 2), op=ALU.add)
-
         def th(i):
-            src = st[("cd", i)] if vector_adds_x(i) else st[("mn", i)]
-            nc.scalar.activation(out=st[("cd", i)][:], in_=src[:], func=FN.Tanh)
+            cnd = work.tile([P, C], F32, name="cnd", tag="cd", bufs=6)
+            nc.scalar.activation(out=cnd[:], in_=st[("mn", i)][:], func=FN.Tanh)
+            st[("cd", i)] = cnd
 
         def mix_engine(i):
             return nc.vector if i >= NT - 2 else nc.gpsimd
@@ -273,43 +263,41 @@ def tile_gatedgraphconvolution_pb_t_kernel(tc, x_proj, annotations, recurrent_ke
         load_h(1)
         load_x(1)
         regroup_w(1, nc.vector.tensor_copy)
-        regroup_w(2, nc.vector.tensor_copy)
+        quantise_w(1)
         b_rows32 = const.tile([P, P], F32)
         b_col = const.tile([P, G // P], F32)
 
         for k in range(-3, NT + 5):
-            run(v, k - 4)
-            run(mxz, k)
-            run(u, k - 3)
-            run(mxr, k + 1)
-            run(sr, k - 1)
-            run(ht, k + 3)
-            run(tz, k - 3)
-            if k == -3:
-                quantise_w(1)
-            run(ac, k - 2)
-            run(q, k + 2)
-            if k == -2:
-                regroup_w(0, nc.vector.tensor_copy)
-            run(ta, k - 1)
-            run(m, k - 1)
-            if k == 0:
-                quantise_w(2)
-                nc.vector.tensor_copy(out=b_col[:], in_=b_ps[:, 0 : G // P])
-            run(tb, k)
-            run(th, k - 2)
-            run(a0, k)
-            run(ev, k + 3)
             if k == -1:
                 quantise_w(0)
                 nc.vector.tensor_copy(out=b_rows32[:], in_=b_rows[:])
+                quantise_w(2)
                 b_ps = psum.tile([P, C], F32, name="b_ps", tag="bt")
                 nc.tensor.transpose(b_ps[:, 0:P], b_rows32[:], ident[:])
-            run(o, k - 5)
+            if k == 0:
+                nc.vector.tensor_copy(out=b_col[:], in_=b_ps[:, 0 : G // P])
+            run(ev, k + 2)
+            run(v, k - 4)
+            run(sr, k - 1)
+            run(tm, k - 2)
+            run(tz, k - 3)
+            run(ta, k - 1)
+            run(ht, k + 3)
+            run(th, k - 2)
+            run(u, k - 3)
+            run(b0, k)
+            run(tb, k)
+            run(m, k - 1)
             run(sz, k - 1)
-            run(b0, k + 1)
-            run(tm, k - 1)
+            run(a0, k)
+            run(mxr, k + 1)
             run(mxc, k)
+            run(q, k + 2)
+            if k == -2:
+                regroup_w(2, nc.scalar.copy)
+                regroup_w(0, nc.vector.tensor_copy)
+            run(mxz, k + 1)
+            run(o, k - 4)
             if (k + 7) % TPB == 0 and 2 <= (k + 7) // TPB < NBLK:
                 load_h((k + 7) // TPB)
                 load_x((k + 7) // TPB)

@@ -128,7 +128,7 @@ def tile_gatedgraphconvolution_pb_t_kernel(tc, x_proj, annotations, recurrent_ke
 
         def ev(i):
             h_grp = qpool.tile([P, 4 * P], BF16, name="h_grp", tag="h_grp", align_bytes=64)
-            nc.vector.tensor_copy(
+            nc.scalar.copy(
                 out=h_grp[:].bitcast(F32).rearrange("q (p u) -> q p u", u=2),
                 in_=st[("xt", i)][:].rearrange("q u p -> q p u"),
             )
@@ -215,7 +215,7 @@ def tile_gatedgraphconvolution_pb_t_kernel(tc, x_proj, annotations, recurrent_ke
             st[("cd", i)] = cnd
 
         def mix_engine(i):
-            return nc.vector if i >= NT - 2 else nc.gpsimd
+            return nc.vector if (i % 8 == 7 or i >= NT - 2) else nc.gpsimd
 
         def u(i):
             u_t = work.tile([P, C], F32, name="u_t", tag="u", bufs=5)

from contextlib import ExitStack

import concourse.mybir as mybir
from concourse.masks import make_identity

F32 = mybir.dt.float32
BF16 = mybir.dt.bfloat16
U32 = mybir.dt.uint32
U8 = mybir.dt.uint8
I32 = mybir.dt.int32
FP8X4 = mybir.dt.float8_e4m3fn_x4
ALU = mybir.AluOpType
FN = mybir.ActivationFunctionType

P = 128
C = 512
G = 3 * C
R = 4096
TPB = 4
NFC = C // P
BLOCK = P * TPB
NBLK = R // BLOCK

FLOPS = 2 * R * C * G
NT = R // P


def tile_gatedgraphconvolution_pb_t_kernel(tc, x_proj, annotations, recurrent_kernel, bias_h, out):
    nc = tc.nc
    h_all = annotations.flatten_outer_dims()
    out_all = out.flatten_outer_dims()

    with ExitStack() as ctx:
        ctx.enter_context(tc.manual_schedule())
        const = ctx.enter_context(tc.tile_pool(name="const", bufs=1))
        xpool = ctx.enter_context(tc.tile_pool(name="xpool", bufs=3))
        hpool = ctx.enter_context(tc.tile_pool(name="hpool", bufs=4))
        qpool = ctx.enter_context(tc.tile_pool(name="qpool", bufs=4))
        work = ctx.enter_context(tc.tile_pool(name="work", bufs=4))
        opool = ctx.enter_context(tc.tile_pool(name="opool", bufs=3))
        psum = ctx.enter_context(tc.psum_pool(name="psum", bufs=1))

        h_blks = {}
        x_blks = {}
        o_blks = {}
        st = {}

        def load_h(b):
            rows = slice(BLOCK * b, BLOCK * b + BLOCK)
            h_blks[b] = hpool.tile([P, TPB * C], BF16, name="h_blk", tag="h_blk")
            nc.sync.dma_start(out=h_blks[b][:], in_=h_all[rows, :].rearrange("(p t) c -> p (t c)", t=TPB))

        def load_x(b):
            src = x_proj[BLOCK * b : BLOCK * b + BLOCK, :].rearrange("(p t) c -> p t c", t=TPB)
            x_blks[b] = xpool.tile([P, TPB, G], BF16, name="x_blk", tag="x_blk")
            for half in range(2):
                ts = slice(2 * half, 2 * half + 2)
                nc.sync.dma_start(out=x_blks[b][:, ts, :], in_=src[:, ts, :])

        def load_w(g):
            cs = slice(C * g, C * g + C)
            for u in range(2):
                nc.sync.dma_start(
                    out=w_raw[:, 2 * u : 2 * u + 2, cs],
                    in_=recurrent_kernel[256 * u : 256 * u + 256, cs].rearrange("(q e) c -> q e c", e=2),
                )

        def regroup_w(g, copy):
            cs = slice(C * g, C * g + C)
            copy(out=w_grp[:, cs, :], in_=w_raw[:, :, cs].rearrange("q t c -> q c t"))

        def quantise_w(g):
            cs = slice(C * g, C * g + C)
            nc.vector.quantize_mx(
                out=w_codes[:, cs].bitcast(FP8X4),
                scales=w_scales[:, cs],
                in_=w_grp[:, cs, :].rearrange("q c t -> q (c t)"),
            )

        def x_of(i, g):
            return x_blks[i // TPB][:, i % TPB, C * g : C * g + C]

        def h_of(i):
            t = i % TPB
            return h_blks[i // TPB][:, C * t : C * t + C]

        def flip(src, tag):
            ps = psum.tile([P, C], F32, name="ps_" + tag, tag=tag)
            for j in range(NFC):
                nc.tensor.transpose(ps[:, P * j : P * j + P], src[:, P * j : P * j + P], ident[:])
            return ps

        def mx_nodes(i, g):
            cs = slice(C * g, C * g + C)
            pg = psum.tile([P, C], F32, name="pg", tag="p%d" % g)
            nc.tensor.matmul_mx(
                out=pg[:],
                lhsT=st[("hc", i)][:].bitcast(FP8X4),
                lhsT_scale=st[("hs", i)][:],
                rhs=w_codes[:, cs].bitcast(FP8X4),
                rhs_scale=w_scales[:, cs],
                start=True,
                stop=True,
            )
            st[("p", g, i)] = pg

        def add_x(i, g):
            s = work.tile([P, C], F32, name="s", tag="s%d" % g)
            nc.vector.tensor_tensor(out=s[:], in0=st[("p", g, i)][:], in1=x_of(i, g), op=ALU.add)
            st[("s", g, i)] = s

        def sigmoid(i, g, bufs):
            ps = st[("sT", g, i)]
            s = work.tile([P, C], F32, name="sg", tag="sg%d" % g, bufs=bufs)
            for fc in range(NFC):
                fs = slice(P * fc, P * fc + P)
                nc.scalar.activation(
                    out=s[:, fs], in_=ps[:, fs], func=FN.Sigmoid, bias=b_col[:, NFC * g + fc : NFC * g + fc + 1]
                )
            st[("gT", g, i)] = s

        def ht(i):
            h_words = h_of(i).bitcast(F32)
            xt = psum.tile([P, 2, P], F32, name="xt", tag="xt")
            for u in range(2):
                nc.tensor.transpose(xt[:, u, :], h_words[:, P * u : P * u + P], ident[:])
            st[("xt", i)] = xt

        def ev(i):
            h_grp = qpool.tile([P, 4 * P], BF16, name="h_grp", tag="h_grp", align_bytes=64)
            nc.scalar.copy(
                out=h_grp[:].bitcast(F32).rearrange("q (p u) -> q p u", u=2),
                in_=st[("xt", i)][:].rearrange("q u p -> q p u"),
            )
            st[("grp", i)] = h_grp

        def q(i):
            h_codes = qpool.tile([P, P], U32, name="h_codes", tag="h_codes", bufs=8, align_bytes=64)
            h_scales = qpool.tile([P, P], U8, name="h_scales", tag="h_scales", bufs=8, align_bytes=64)
            nc.vector.quantize_mx(out=h_codes[:].bitcast(FP8X4), scales=h_scales[:], in_=st[("grp", i)][:])
            st[("hc", i)] = h_codes
            st[("hs", i)] = h_scales

        def mxr(i):
            mx_nodes(i, 1)

        def mxz(i):
            mx_nodes(i, 0)

        def mxc(i):
            pc = psum.tile([P, C], F32, name="pc", tag="pc")
            for fc in range(NFC):
                cs = slice(2 * C + P * fc, 2 * C + P * fc + P)
                nc.tensor.matmul_mx(
                    out=pc[:, P * fc : P * fc + P],
                    lhsT=w_codes[:, cs].bitcast(FP8X4),
                    lhsT_scale=w_scales[:, cs],
                    rhs=st[("hc", i)][:].bitcast(FP8X4),
                    rhs_scale=st[("hs", i)][:],
                    start=True,
                    stop=True,
                )
            st[("pc", i)] = pc

        def b0(i):
            add_x(i, 1)

        def a0(i):
            add_x(i, 0)

        def tb(i):
            st[("sT", 1, i)] = flip(st[("s", 1, i)], "bt")

        def ta(i):
            st[("sT", 0, i)] = flip(st[("s", 0, i)], "at")

        def sr(i):
            sigmoid(i, 1, 4)

        def sz(i):
            sigmoid(i, 0, 6)

        def m(i):
            m_t = work.tile([P, C], F32, name="m_t", tag="mT")
            for fc in range(NFC):
                fs = slice(P * fc, P * fc + P)
                nc.vector.scalar_tensor_tensor(
                    out=m_t[:, fs],
                    in0=st[("pc", i)][:, fs],
                    scalar=b_col[:, 2 * NFC + fc : 2 * NFC + fc + 1],
                    in1=st[("gT", 1, i)][:, fs],
                    op0=ALU.add,
                    op1=ALU.mult,
                )
            st[("m", i)] = m_t

        def tm(i):
            mn = psum.tile([P, C], F32, name="mn", tag="mn")
            nc.tensor.matmul(out=mn[:], lhsT=ident_bf[:], rhs=x_of(i, 2), start=True, stop=False)
            for j in range(NFC):
                js = slice(P * j, P * j + P)
                nc.tensor.matmul(
                    out=mn[:, js],
                    lhsT=st[("m", i)][:, js],
                    rhs=ident[:],
                    is_transpose=True,
                    start=False,
                    stop=(j == NFC - 1),
                )
            st[("mn", i)] = mn

        def th(i):
            cnd = work.tile([P, C], F32, name="cnd", tag="cd", bufs=6)
            nc.scalar.activation(out=cnd[:], in_=st[("mn", i)][:], func=FN.Tanh)
            st[("cd", i)] = cnd

        def mix_engine(i):
            return nc.vector if (i % 8 == 7 or i >= NT - 2) else nc.gpsimd

        def u(i):
            u_t = work.tile([P, C], F32, name="u_t", tag="u", bufs=5)
            mix_engine(i).tensor_tensor(out=u_t[:], in0=h_of(i), in1=st[("cd", i)][:], op=ALU.subtract)
            st[("u", i)] = u_t

        def tz(i):
            st[("zn", i)] = flip(st[("gT", 0, i)], "zn")

        def v(i):
            nc.vector.tensor_tensor(out=st[("u", i)][:], in0=st[("zn", i)][:], in1=st[("u", i)][:], op=ALU.mult)

        def o(i):
            b = i // TPB
            t = i % TPB
            if t == 0:
                o_blks[b] = opool.tile([P, TPB, C], F32, name="o_blk", tag="o_blk")
            mix_engine(i).tensor_tensor(out=o_blks[b][:, t, :], in0=st[("u", i)][:], in1=st[("cd", i)][:], op=ALU.add)
            dst = out_all[BLOCK * b : BLOCK * b + BLOCK, :].rearrange("(p t) c -> p t c", t=TPB)
            if b == NBLK - 1:
                nc.sync.dma_start(out=dst[:, t, :], in_=o_blks[b][:, t, :])
            elif t == TPB - 1:
                nc.sync.dma_start(out=dst, in_=o_blks[b][:])

        def run(stage, i):
            if 0 <= i < NT:
                stage(i)

        b_rows = const.tile([P, P], BF16)
        nc.vector.memset(b_rows[:].bitcast(I32), 0)
        nc.scalar.dma_start(out=b_rows[0 : G // P, :], in_=bias_h.rearrange("(j q) -> j q", q=P))
        ident = const.tile([P, P], F32)
        make_identity(nc, ident[:])
        ident_bf = const.tile([P, P], BF16)
        make_identity(nc, ident_bf[:])
        w_raw = const.tile([P, 4, G], BF16)
        w_grp = const.tile([P, G, 4], BF16, align_bytes=64)
        w_codes = const.tile([P, G], U32, align_bytes=64)
        w_scales = const.tile([P, G], U8, align_bytes=64)
        load_w(1)
        load_h(0)
        load_w(2)
        load_w(0)
        load_x(0)
        load_h(1)
        load_x(1)
        regroup_w(1, nc.vector.tensor_copy)
        quantise_w(1)
        b_rows32 = const.tile([P, P], F32)
        b_col = const.tile([P, G // P], F32)

        for k in range(-3, NT + 5):
            if k == -1:
                quantise_w(0)
                nc.vector.tensor_copy(out=b_rows32[:], in_=b_rows[:])
                quantise_w(2)
                b_ps = psum.tile([P, C], F32, name="b_ps", tag="bt")
                nc.tensor.transpose(b_ps[:, 0:P], b_rows32[:], ident[:])
            if k == 0:
                nc.vector.tensor_copy(out=b_col[:], in_=b_ps[:, 0 : G // P])
            run(ev, k + 2)
            run(v, k - 4)
            run(sr, k - 1)
            run(tm, k - 2)
            run(tz, k - 3)
            run(ta, k - 1)
            run(ht, k + 3)
            run(th, k - 2)
            run(u, k - 3)
            run(b0, k)
            run(tb, k)
            run(m, k - 1)
            run(sz, k - 1)
            run(a0, k)
            run(mxr, k + 1)
            run(mxc, k)
            run(q, k + 2)
            if k == -2:
                regroup_w(2, nc.scalar.copy)
                regroup_w(0, nc.vector.tensor_copy)
            run(mxz, k + 1)
            run(o, k - 4)
            if (k + 7) % TPB == 0 and 2 <= (k + 7) // TPB < NBLK:
                load_h((k + 7) // TPB)
                load_x((k + 7) // TPB)
